import numpy as np
import ml_dtypes


def mxq(x, axis, fmt="e4m3"):
    dtype, down = {"e4m3": (ml_dtypes.float8_e4m3fn, 7), "e5m2": (ml_dtypes.float8_e5m2, 14)}[fmt]
    v = np.moveaxis(np.asarray(x, np.float32).astype(ml_dtypes.bfloat16).astype(np.float64), axis, -1)
    blocks = v.reshape(v.shape[:-1] + (-1, 32))
    amax = np.abs(blocks).max(-1, keepdims=True)
    byte = np.maximum(np.where(amax > 0, np.frexp(amax)[1] - 1 + 127, 0) - down, 1)
    scale = np.exp2(byte - 127.0)
    codes = (blocks / scale).astype(np.float32).astype(dtype).astype(np.float64)
    return np.moveaxis((codes * scale).reshape(v.shape), -1, axis)


WIDE = False


def mx_kscale(k):
    if not WIDE:
        return np.ones(k)
    levels = np.array([10, -10, 5, -5, 0])
    a = np.random.permutation(np.resize(levels, k // 512 * 4)).reshape(k // 512, 4)
    idx = np.arange(k)
    return np.exp2(a[idx // 512, idx % 128 // 32])


BF16 = ml_dtypes.bfloat16


def bf(x):
    return np.asarray(x, np.float32).astype(BF16)


def f64(x):
    return np.asarray(x).astype(np.float64)


B, L, E, QH, KVH, D, FFN = 2, 2048, 512, 8, 1, 128, 1024
KV = KVH * D
EPS = 1.1920928955078125e-07


def rmsnorm(x, w):
    return x / np.sqrt(np.mean(x * x, axis=-1, keepdims=True) + EPS) * w


def setup_inputs():
    s, t = mx_kscale(FFN), mx_kscale(E)
    return {"ffn_act": bf(np.random.standard_normal((B, L, FFN)) * 0.6 * s),
            "wd": bf(np.random.standard_normal((FFN, E)) / np.sqrt(FFN) / s[:, None]),
            "residual": bf(np.random.standard_normal((B, L, E)) * 1.1),
            "ln1_w": bf((1.0 + 0.1 * np.random.standard_normal(E)) * t),
            "wk": bf(np.random.standard_normal((E, KV)) / np.sqrt(E) / t[:, None]),
            "wv": bf(np.random.standard_normal((E, KV)) / np.sqrt(E) / t[:, None])}


def reference(ffn_act, wd, residual, ln1_w, wk, wv):
    x_out = (mxq(f64(ffn_act), 2, "e4m3") @ mxq(f64(wd), 0, "e4m3")) + f64(residual)
    hq = mxq(rmsnorm(x_out, f64(ln1_w)), 2, "e4m3")
    k_out = (hq @ mxq(f64(wk), 0, "e4m3")).reshape(B, L, KV)
    v_out = (hq @ mxq(f64(wv), 0, "e4m3")).reshape(B, L, KV)
    return x_out, k_out, v_out

@@ -1,0 +1,309 @@
+from contextlib import ExitStack
+
+import concourse.mybir as mybir
+from concourse.masks import make_identity
+
+F32 = mybir.dt.float32
+BF16 = mybir.dt.bfloat16
+U32 = mybir.dt.uint32
+U8 = mybir.dt.uint8
+FP8X4 = mybir.dt.float8_e4m3fn_x4
+ACT = mybir.ActivationFunctionType
+ALU = mybir.AluOpType
+
+P = 128
+PACK = 4
+K_PASS = P * PACK
+
+TOKENS = 4096
+FFN = 1024
+E = 512
+KV = 128
+EPS = 2.0**-23
+DOWN_PASSES = FFN // K_PASS
+
+CHUNK_TILES = 4
+CHUNK = CHUNK_TILES * P
+GROUP = 2
+ROUNDS = TOKENS // (GROUP * P)
+ROUNDS_PER_CHUNK = CHUNK_TILES // GROUP
+LOADS_AHEAD = 4
+
+FLOPS = 2 * TOKENS * FFN * E + 2 * TOKENS * E * (2 * KV)
+
+
+def tile_textencoderblock_pc_t_kernel(
+    tc, ffn_act, wd, residual, ln1_w, wk, wv, out_0, out_1, out_2
+):
+    nc = tc.nc
+    a_rows = ffn_act.flatten_outer_dims()
+    res_rows = residual.flatten_outer_dims()
+    x_rows = out_0.flatten_outer_dims()
+    k_rows = out_1.flatten_outer_dims()
+    v_rows = out_2.flatten_outer_dims()
+
+    def chunk_view(rows, c):
+        return rows[c * CHUNK : (c + 1) * CHUNK, :].rearrange("(p j) w -> p j w", j=CHUNK_TILES)
+
+    def first_tile(r):
+        return GROUP * (r % ROUNDS_PER_CHUNK)
+
+    def round_view(rows, r):
+        j0 = first_tile(r)
+        return chunk_view(rows, r // ROUNDS_PER_CHUNK)[:, j0 : j0 + GROUP, :]
+
+    with ExitStack() as ctx:
+        consts = ctx.enter_context(tc.tile_pool(name="consts", bufs=1))
+        a_pool = ctx.enter_context(tc.tile_pool(name="a", bufs=LOADS_AHEAD + 2))
+        res_pool = ctx.enter_context(tc.tile_pool(name="res", bufs=5))
+        grouped_pool = ctx.enter_context(tc.tile_pool(name="grouped", bufs=2))
+        mx_pool = ctx.enter_context(tc.tile_pool(name="mx", bufs=2))
+        x_pool = ctx.enter_context(tc.tile_pool(name="x", bufs=3))
+        stat_pool = ctx.enter_context(tc.tile_pool(name="stat", bufs=3))
+        square_pool = ctx.enter_context(tc.tile_pool(name="square", bufs=4))
+        h_pool = ctx.enter_context(tc.tile_pool(name="h", bufs=2))
+        kv_pool = ctx.enter_context(tc.tile_pool(name="kv", bufs=2))
+        psum_a = ctx.enter_context(tc.psum_pool(name="psum_a", bufs=3))
+        psum_x = ctx.enter_context(tc.psum_pool(name="psum_x", bufs=3))
+        psum_h = ctx.enter_context(tc.psum_pool(name="psum_h", bufs=1))
+        psum_kv = ctx.enter_context(tc.psum_pool(name="psum_kv", bufs=1))
+        ctx.enter_context(tc.manual_schedule())
+
+        a_of, res_of, aT_of, a_grouped_of, a_mx_of, x_psum_of = {}, {}, {}, {}, {}, {}
+        x_of, std_of, h_of, hT_of, h_grouped_of, h_mx_of, kv_psum_of, kv_of = {}, {}, {}, {}, {}, {}, {}, {}
+
+        ident = consts.tile([P, P], F32)
+        make_identity(nc, ident[:])
+        ones = consts.tile([P, P], BF16)
+        nc.vector.memset(ones[:], 1.0)
+        gain_row = consts.tile([P, E], BF16)
+        nc.vector.memset(gain_row[:], 0.0)
+        eps_col = consts.tile([P, 1], F32)
+        nc.vector.memset(eps_col[:], EPS)
+        table_warmer = consts.tile([P, 1], F32)
+        nc.scalar.activation(out=table_warmer[:], in_=eps_col[:], func=ACT.Sqrt)
+
+        def load_weight_pass(rows, raw):
+            nc.sync.dma_start(
+                out=raw.rearrange("p (u e) n -> p u (e n)", e=2),
+                in_=rows.rearrange("(u p e) n -> p u (e n)", u=2, e=2),
+            )
+
+        def load_round(r):
+            a_sb = a_pool.tile([P, GROUP, FFN], BF16)
+            nc.sync.dma_start(out=a_sb[:], in_=round_view(a_rows, r))
+            a_of[r] = a_sb
+            if r % ROUNDS_PER_CHUNK == 0:
+                res_sb = res_pool.tile([P, CHUNK_TILES, E], BF16)
+                nc.sync.dma_start(out=res_sb[:], in_=chunk_view(res_rows, r // ROUNDS_PER_CHUNK))
+                res_of[r // ROUNDS_PER_CHUNK] = res_sb
+
+        wd_raw = consts.tile([P, DOWN_PASSES, PACK, E], BF16)
+        wkv_raw = consts.tile([P, 2, PACK, KV], BF16)
+        nc.sync.dma_start(out=gain_row[0:1, :], in_=ln1_w.unsqueeze(0))
+        load_weight_pass(wd[0:K_PASS, :], wd_raw[:, 0])
+        load_round(0)
+        load_weight_pass(wd[K_PASS : 2 * K_PASS, :], wd_raw[:, 1])
+        load_weight_pass(wk, wkv_raw[:, 0])
+        load_weight_pass(wv, wkv_raw[:, 1])
+        for r in range(1, LOADS_AHEAD):
+            load_round(r)
+
+        gain_psum = psum_x.tile([P, E], F32, tag="x_psum")
+        nc.tensor.matmul(out=gain_psum[:], lhsT=ones[:], rhs=gain_row[:], start=True, stop=True)
+        gain = consts.tile([P, E], F32)
+        nc.scalar.copy(out=gain[:], in_=gain_psum[:])
+
+        def group_weight(raw, grouped):
+            nc.vector.tensor_copy(
+                out=grouped.rearrange("p (c i) t -> p c t i", i=4),
+                in_=raw.rearrange("p t (c i) -> p c t i", i=4),
+            )
+
+        wd_grouped = consts.tile([P, DOWN_PASSES, E, PACK], BF16, align_bytes=64)
+        wd_codes = consts.tile([P, DOWN_PASSES, E], U32, align_bytes=64)
+        wd_scales = consts.tile([P, DOWN_PASSES, E], U8, align_bytes=64)
+        for g in range(DOWN_PASSES):
+            group_weight(wd_raw[:, g], wd_grouped[:, g])
+            nc.vector.quantize_mx(
+                out=wd_codes[:, g, :].bitcast(FP8X4),
+                scales=wd_scales[:, g, :],
+                in_=wd_grouped[:, g].rearrange("p n t -> p (n t)"),
+            )
+
+        wkv_grouped = consts.tile([P, 2, KV, PACK], BF16, align_bytes=64)
+        wkv_codes = consts.tile([P, 2 * KV], U32, align_bytes=64)
+        wkv_scales = consts.tile([P, 2 * KV], U8, align_bytes=64)
+
+        def quantise_wk_wv():
+            for s in range(2):
+                group_weight(wkv_raw[:, s], wkv_grouped[:, s])
+            nc.vector.quantize_mx(
+                out=wkv_codes[:].bitcast(FP8X4),
+                scales=wkv_scales[:],
+                in_=wkv_grouped[:].rearrange("p s n t -> p (s n t)"),
+            )
+
+        def transpose_a(r):
+            a_words = a_of[r][:].rearrange("p i k -> p (i k)").bitcast(F32)
+            for i in range(GROUP):
+                aT = psum_a.tile([P, PACK * P], F32)
+                for gu in range(PACK):
+                    w0 = (PACK * i + gu) * P
+                    nc.tensor.transpose(aT[:, gu * P : (gu + 1) * P], a_words[:, w0 : w0 + P], ident[:])
+                aT_of[(r, i)] = aT
+
+        def group_a(r):
+            a_grouped = grouped_pool.tile([P, GROUP * FFN], BF16, align_bytes=64)
+            words = a_grouped[:].bitcast(F32).rearrange(
+                "p (i g r u) -> p i g r u", i=GROUP, g=DOWN_PASSES, u=2
+            )
+            for i in range(GROUP):
+                nc.scalar.copy(
+                    out=words[:, i],
+                    in_=aT_of[(r, i)][:].rearrange("p (g u r) -> p g r u", g=DOWN_PASSES, u=2),
+                )
+            a_grouped_of[r] = a_grouped
+
+        def quantise_a(r):
+            a_codes = mx_pool.tile([P, GROUP * DOWN_PASSES * P], U32, align_bytes=64)
+            a_scales = mx_pool.tile([P, GROUP * DOWN_PASSES * P], U8, align_bytes=64)
+            nc.vector.quantize_mx(
+                out=a_codes[:].bitcast(FP8X4), scales=a_scales[:], in_=a_grouped_of[r][:]
+            )
+            a_mx_of[r] = (a_codes, a_scales)
+
+        def project_down(r):
+            a_codes, a_scales = a_mx_of[r]
+            for i in range(GROUP):
+                x_psum = psum_x.tile([P, E], F32, tag="x_psum")
+                for g in range(DOWN_PASSES):
+                    cols = slice((DOWN_PASSES * i + g) * P, (DOWN_PASSES * i + g + 1) * P)
+                    nc.tensor.matmul_mx(
+                        out=x_psum[:],
+                        lhsT=a_codes[:, cols].bitcast(FP8X4),
+                        lhsT_scale=a_scales[:, cols],
+                        rhs=wd_codes[:, g, :].bitcast(FP8X4),
+                        rhs_scale=wd_scales[:, g, :],
+                        start=(g == 0),
+                        stop=(g == DOWN_PASSES - 1),
+                    )
+                x_psum_of[(r, i)] = x_psum
+
+        def add_residual(r):
+            res_sb = res_of[r // ROUNDS_PER_CHUNK]
+            x_sb = x_pool.tile([P, GROUP, E], F32)
+            for i in range(GROUP):
+                nc.vector.tensor_tensor(
+                    out=x_sb[:, i, :],
+                    in0=x_psum_of[(r, i)][:],
+                    in1=res_sb[:, first_tile(r) + i, :],
+                    op=ALU.add,
+                )
+            nc.sync.dma_start(out=round_view(x_rows, r), in_=x_sb[:])
+            x_of[r] = x_sb
+
+        def root_mean_square(r):
+            sum_sq = stat_pool.tile([P, GROUP], F32)
+            for i in range(GROUP):
+                squares = square_pool.tile([P, E], BF16)
+                nc.scalar.activation(
+                    out=squares[:], in_=x_of[r][:, i, :], func=ACT.Square, accum_out=sum_sq[:, i : i + 1]
+                )
+            std = stat_pool.tile([P, GROUP], F32)
+            nc.scalar.activation(out=std[:], in_=sum_sq[:], func=ACT.Sqrt, bias=eps_col[:], scale=1.0 / E)
+            std_of[r] = std
+
+        def normalise(r):
+            rstd = stat_pool.tile([P, GROUP], F32)
+            nc.vector.reciprocal(out=rstd[:], in_=std_of[r][:])
+            h_sb = h_pool.tile([P, GROUP * E], BF16)
+            for i in range(GROUP):
+                nc.vector.scalar_tensor_tensor(
+                    out=h_sb[:, i * E : (i + 1) * E],
+                    in0=x_of[r][:, i, :],
+                    scalar=rstd[:, i : i + 1],
+                    in1=gain[:],
+                    op0=ALU.mult,
+                    op1=ALU.mult,
+                )
+            h_of[r] = h_sb
+
+        def transpose_h(r):
+            h_words = h_of[r][:].bitcast(F32)
+            hT = psum_h.tile([P, GROUP * 2 * P], F32)
+            for iu in range(GROUP * 2):
+                cols = slice(iu * P, (iu + 1) * P)
+                nc.tensor.transpose(hT[:, cols], h_words[:, cols], ident[:])
+            hT_of[r] = hT
+
+        def group_h(r):
+            h_grouped = grouped_pool.tile([P, GROUP * E], BF16, align_bytes=64)
+            nc.scalar.copy(
+                out=h_grouped[:].bitcast(F32).rearrange("p (i r u) -> p i r u", i=GROUP, u=2),
+                in_=hT_of[r][:].rearrange("p (i u r) -> p i r u", i=GROUP, u=2),
+            )
+            h_grouped_of[r] = h_grouped
+
+        def quantise_h(r):
+            h_codes = mx_pool.tile([P, GROUP * P], U32, align_bytes=64)
+            h_scales = mx_pool.tile([P, GROUP * P], U8, align_bytes=64)
+            nc.vector.quantize_mx(
+                out=h_codes[:].bitcast(FP8X4), scales=h_scales[:], in_=h_grouped_of[r][:]
+            )
+            h_mx_of[r] = (h_codes, h_scales)
+
+        def project_kv(r):
+            h_codes, h_scales = h_mx_of[r]
+            kv_psum = psum_kv.tile([P, GROUP, 2 * KV], F32)
+            for i in range(GROUP):
+                cols = slice(i * P, (i + 1) * P)
+                nc.tensor.matmul_mx(
+                    out=kv_psum[:, i, :],
+                    lhsT=h_codes[:, cols].bitcast(FP8X4),
+                    lhsT_scale=h_scales[:, cols],
+                    rhs=wkv_codes[:].bitcast(FP8X4),
+                    rhs_scale=wkv_scales[:],
+                    start=True,
+                    stop=True,
+                )
+            kv_psum_of[r] = kv_psum
+
+        def store_kv(r):
+            c = r // ROUNDS_PER_CHUNK
+            if r % ROUNDS_PER_CHUNK == 0:
+                kv_sb = kv_pool.tile([P, 2, CHUNK_TILES, KV], F32)
+                kv_of[c] = kv_sb
+            j0 = first_tile(r)
+            nc.scalar.copy(
+                out=kv_of[c][:, :, j0 : j0 + GROUP, :],
+                in_=kv_psum_of[r][:].rearrange("p i (s d) -> p s i d", s=2),
+            )
+            if r % ROUNDS_PER_CHUNK == ROUNDS_PER_CHUNK - 1:
+                nc.sync.dma_start(out=chunk_view(k_rows, c), in_=kv_of[c][:, 0])
+                nc.sync.dma_start(out=chunk_view(v_rows, c), in_=kv_of[c][:, 1])
+
+        def run(stage, r):
+            if 0 <= r < ROUNDS:
+                stage(r)
+
+        def frame(f):
+            run(load_round, f + 2 + LOADS_AHEAD)
+            run(transpose_h, f - 2)
+            run(add_residual, f)
+            run(root_mean_square, f)
+            run(transpose_a, f + 2)
+            run(quantise_a, f + 1)
+            run(project_down, f + 1)
+            run(normalise, f - 1)
+            run(group_h, f - 2)
+            run(store_kv, f - 3)
+            run(quantise_h, f - 2)
+            run(project_kv, f - 2)
+            run(group_a, f + 2)
+
+        frame(-2)
+        frame(-1)
+        quantise_wk_wv()
+        for f in range(ROUNDS + 3):
+            frame(f)

@@ -22,12 +22,11 @@ KV = 128
 EPS = 2.0**-23
 DOWN_PASSES = FFN // K_PASS
 
+TILES = TOKENS // P
+PAIR = 2
 CHUNK_TILES = 4
 CHUNK = CHUNK_TILES * P
-GROUP = 2
-ROUNDS = TOKENS // (GROUP * P)
-ROUNDS_PER_CHUNK = CHUNK_TILES // GROUP
-LOADS_AHEAD = 4
+LOADS_AHEAD = 8
 
 FLOPS = 2 * TOKENS * FFN * E + 2 * TOKENS * E * (2 * KV)
 
@@ -45,32 +44,30 @@ def tile_textencoderblock_pc_t_kernel(
     def chunk_view(rows, c):
         return rows[c * CHUNK : (c + 1) * CHUNK, :].rearrange("(p j) w -> p j w", j=CHUNK_TILES)
 
-    def first_tile(r):
-        return GROUP * (r % ROUNDS_PER_CHUNK)
-
-    def round_view(rows, r):
-        j0 = first_tile(r)
-        return chunk_view(rows, r // ROUNDS_PER_CHUNK)[:, j0 : j0 + GROUP, :]
+    def pair_view(rows, s):
+        j0 = s % CHUNK_TILES
+        return chunk_view(rows, s // CHUNK_TILES)[:, j0 : j0 + PAIR, :]
 
     with ExitStack() as ctx:
         consts = ctx.enter_context(tc.tile_pool(name="consts", bufs=1))
-        a_pool = ctx.enter_context(tc.tile_pool(name="a", bufs=LOADS_AHEAD + 2))
+        a_pool = ctx.enter_context(tc.tile_pool(name="a", bufs=LOADS_AHEAD // PAIR + 2))
         res_pool = ctx.enter_context(tc.tile_pool(name="res", bufs=5))
         grouped_pool = ctx.enter_context(tc.tile_pool(name="grouped", bufs=2))
         mx_pool = ctx.enter_context(tc.tile_pool(name="mx", bufs=2))
-        x_pool = ctx.enter_context(tc.tile_pool(name="x", bufs=3))
-        stat_pool = ctx.enter_context(tc.tile_pool(name="stat", bufs=3))
+        x_pool = ctx.enter_context(tc.tile_pool(name="x", bufs=4))
+        stat_pool = ctx.enter_context(tc.tile_pool(name="stat", bufs=4))
         square_pool = ctx.enter_context(tc.tile_pool(name="square", bufs=4))
         h_pool = ctx.enter_context(tc.tile_pool(name="h", bufs=2))
         kv_pool = ctx.enter_context(tc.tile_pool(name="kv", bufs=2))
-        psum_a = ctx.enter_context(tc.psum_pool(name="psum_a", bufs=3))
-        psum_x = ctx.enter_context(tc.psum_pool(name="psum_x", bufs=3))
+        psum_gain = ctx.enter_context(tc.psum_pool(name="psum_gain", bufs=1))
+        psum_a = ctx.enter_context(tc.psum_pool(name="psum_a", bufs=2))
+        psum_x = ctx.enter_context(tc.psum_pool(name="psum_x", bufs=2))
         psum_h = ctx.enter_context(tc.psum_pool(name="psum_h", bufs=1))
-        psum_kv = ctx.enter_context(tc.psum_pool(name="psum_kv", bufs=1))
+        psum_kv = ctx.enter_context(tc.psum_pool(name="psum_kv", bufs=2))
         ctx.enter_context(tc.manual_schedule())
 
-        a_of, res_of, aT_of, a_grouped_of, a_mx_of, x_psum_of = {}, {}, {}, {}, {}, {}
-        x_of, std_of, h_of, hT_of, h_grouped_of, h_mx_of, kv_psum_of, kv_of = {}, {}, {}, {}, {}, {}, {}, {}
+        a_of, res_of, aT_of, a_grouped_of, a_mx_of, x_psum_of, x_of = {}, {}, {}, {}, {}, {}, {}
+        rstd_of, h_of, hT_of, h_grouped_of, h_mx_of, kv_psum_of, kv_of = {}, {}, {}, {}, {}, {}, {}
 
         ident = consts.tile([P, P], F32)
         make_identity(nc, ident[:])
@@ -78,10 +75,10 @@ def tile_textencoderblock_pc_t_kernel(
         nc.vector.memset(ones[:], 1.0)
         gain_row = consts.tile([P, E], BF16)
         nc.vector.memset(gain_row[:], 0.0)
-        eps_col = consts.tile([P, 1], F32)
-        nc.vector.memset(eps_col[:], EPS)
+        minus_half = consts.tile([P, 1], F32)
+        nc.vector.memset(minus_half[:], -0.5)
         table_warmer = consts.tile([P, 1], F32)
-        nc.scalar.activation(out=table_warmer[:], in_=eps_col[:], func=ACT.Sqrt)
+        nc.scalar.activation(out=table_warmer[:], in_=minus_half[:], func=ACT.Square)
 
         def load_weight_pass(rows, raw):
             nc.sync.dma_start(
@@ -89,30 +86,29 @@ def tile_textencoderblock_pc_t_kernel(
                 in_=rows.rearrange("(u p e) n -> p u (e n)", u=2, e=2),
             )
 
-        def load_round(r):
-            a_sb = a_pool.tile([P, GROUP, FFN], BF16)
-            nc.sync.dma_start(out=a_sb[:], in_=round_view(a_rows, r))
-            a_of[r] = a_sb
-            if r % ROUNDS_PER_CHUNK == 0:
+        def load_inputs(s):
+            if s % PAIR == 0:
+                a_sb = a_pool.tile([P, PAIR, FFN], BF16)
+                nc.sync.dma_start(out=a_sb[:], in_=pair_view(a_rows, s))
+                a_of[s // PAIR] = a_sb
+            if s % CHUNK_TILES == 0:
                 res_sb = res_pool.tile([P, CHUNK_TILES, E], BF16)
-                nc.sync.dma_start(out=res_sb[:], in_=chunk_view(res_rows, r // ROUNDS_PER_CHUNK))
-                res_of[r // ROUNDS_PER_CHUNK] = res_sb
+                nc.sync.dma_start(out=res_sb[:], in_=chunk_view(res_rows, s // CHUNK_TILES))
+                res_of[s // CHUNK_TILES] = res_sb
 
         wd_raw = consts.tile([P, DOWN_PASSES, PACK, E], BF16)
         wkv_raw = consts.tile([P, 2, PACK, KV], BF16)
         nc.sync.dma_start(out=gain_row[0:1, :], in_=ln1_w.unsqueeze(0))
-        load_weight_pass(wd[0:K_PASS, :], wd_raw[:, 0])
-        load_round(0)
-        load_weight_pass(wd[K_PASS : 2 * K_PASS, :], wd_raw[:, 1])
+        for g in range(DOWN_PASSES):
+            load_weight_pass(wd[g * K_PASS : (g + 1) * K_PASS, :], wd_raw[:, g])
+        load_inputs(0)
         load_weight_pass(wk, wkv_raw[:, 0])
         load_weight_pass(wv, wkv_raw[:, 1])
-        for r in range(1, LOADS_AHEAD):
-            load_round(r)
+        for s in range(1, LOADS_AHEAD):
+            load_inputs(s)
 
-        gain_psum = psum_x.tile([P, E], F32, tag="x_psum")
-        nc.tensor.matmul(out=gain_psum[:], lhsT=ones[:], rhs=gain_row[:], start=True, stop=True)
-        gain = consts.tile([P, E], F32)
-        nc.scalar.copy(out=gain[:], in_=gain_psum[:])
+        gain = psum_gain.tile([P, E], F32)
+        nc.tensor.matmul(out=gain[:], lhsT=ones[:], rhs=gain_row[:], start=True, stop=True)
 
         def group_weight(raw, grouped):
             nc.vector.tensor_copy(
@@ -125,6 +121,7 @@ def tile_textencoderblock_pc_t_kernel(
         wd_scales = consts.tile([P, DOWN_PASSES, E], U8, align_bytes=64)
         for g in range(DOWN_PASSES):
             group_weight(wd_raw[:, g], wd_grouped[:, g])
+        for g in range(DOWN_PASSES):
             nc.vector.quantize_mx(
                 out=wd_codes[:, g, :].bitcast(FP8X4),
                 scales=wd_scales[:, g, :],
@@ -144,166 +141,157 @@ def tile_textencoderblock_pc_t_kernel(
                 in_=wkv_grouped[:].rearrange("p s n t -> p (s n t)"),
             )
 
-        def transpose_a(r):
-            a_words = a_of[r][:].rearrange("p i k -> p (i k)").bitcast(F32)
-            for i in range(GROUP):
-                aT = psum_a.tile([P, PACK * P], F32)
-                for gu in range(PACK):
-                    w0 = (PACK * i + gu) * P
-                    nc.tensor.transpose(aT[:, gu * P : (gu + 1) * P], a_words[:, w0 : w0 + P], ident[:])
-                aT_of[(r, i)] = aT
+        def transpose_a(s):
+            a_words = a_of[s // PAIR][:, s % PAIR, :].bitcast(F32)
+            aT = psum_a.tile([P, PACK * P], F32)
+            for gu in range(PACK):
+                cols = slice(gu * P, (gu + 1) * P)
+                nc.tensor.transpose(aT[:, cols], a_words[:, cols], ident[:])
+            aT_of[s] = aT
 
-        def group_a(r):
-            a_grouped = grouped_pool.tile([P, GROUP * FFN], BF16, align_bytes=64)
-            words = a_grouped[:].bitcast(F32).rearrange(
-                "p (i g r u) -> p i g r u", i=GROUP, g=DOWN_PASSES, u=2
-            )
-            for i in range(GROUP):
-                nc.scalar.copy(
-                    out=words[:, i],
-                    in_=aT_of[(r, i)][:].rearrange("p (g u r) -> p g r u", g=DOWN_PASSES, u=2),
-                )
-            a_grouped_of[r] = a_grouped
-
-        def quantise_a(r):
-            a_codes = mx_pool.tile([P, GROUP * DOWN_PASSES * P], U32, align_bytes=64)
-            a_scales = mx_pool.tile([P, GROUP * DOWN_PASSES * P], U8, align_bytes=64)
-            nc.vector.quantize_mx(
-                out=a_codes[:].bitcast(FP8X4), scales=a_scales[:], in_=a_grouped_of[r][:]
-            )
-            a_mx_of[r] = (a_codes, a_scales)
-
-        def project_down(r):
-            a_codes, a_scales = a_mx_of[r]
-            for i in range(GROUP):
-                x_psum = psum_x.tile([P, E], F32, tag="x_psum")
-                for g in range(DOWN_PASSES):
-                    cols = slice((DOWN_PASSES * i + g) * P, (DOWN_PASSES * i + g + 1) * P)
-                    nc.tensor.matmul_mx(
-                        out=x_psum[:],
-                        lhsT=a_codes[:, cols].bitcast(FP8X4),
-                        lhsT_scale=a_scales[:, cols],
-                        rhs=wd_codes[:, g, :].bitcast(FP8X4),
-                        rhs_scale=wd_scales[:, g, :],
-                        start=(g == 0),
-                        stop=(g == DOWN_PASSES - 1),
-                    )
-                x_psum_of[(r, i)] = x_psum
-
-        def add_residual(r):
-            res_sb = res_of[r // ROUNDS_PER_CHUNK]
-            x_sb = x_pool.tile([P, GROUP, E], F32)
-            for i in range(GROUP):
-                nc.vector.tensor_tensor(
-                    out=x_sb[:, i, :],
-                    in0=x_psum_of[(r, i)][:],
-                    in1=res_sb[:, first_tile(r) + i, :],
-                    op=ALU.add,
-                )
-            nc.sync.dma_start(out=round_view(x_rows, r), in_=x_sb[:])
-            x_of[r] = x_sb
-
-        def root_mean_square(r):
-            sum_sq = stat_pool.tile([P, GROUP], F32)
-            for i in range(GROUP):
-                squares = square_pool.tile([P, E], BF16)
-                nc.scalar.activation(
-                    out=squares[:], in_=x_of[r][:, i, :], func=ACT.Square, accum_out=sum_sq[:, i : i + 1]
-                )
-            std = stat_pool.tile([P, GROUP], F32)
-            nc.scalar.activation(out=std[:], in_=sum_sq[:], func=ACT.Sqrt, bias=eps_col[:], scale=1.0 / E)
-            std_of[r] = std
-
-        def normalise(r):
-            rstd = stat_pool.tile([P, GROUP], F32)
-            nc.vector.reciprocal(out=rstd[:], in_=std_of[r][:])
-            h_sb = h_pool.tile([P, GROUP * E], BF16)
-            for i in range(GROUP):
-                nc.vector.scalar_tensor_tensor(
-                    out=h_sb[:, i * E : (i + 1) * E],
-                    in0=x_of[r][:, i, :],
-                    scalar=rstd[:, i : i + 1],
-                    in1=gain[:],
-                    op0=ALU.mult,
-                    op1=ALU.mult,
-                )
-            h_of[r] = h_sb
-
-        def transpose_h(r):
-            h_words = h_of[r][:].bitcast(F32)
-            hT = psum_h.tile([P, GROUP * 2 * P], F32)
-            for iu in range(GROUP * 2):
-                cols = slice(iu * P, (iu + 1) * P)
-                nc.tensor.transpose(hT[:, cols], h_words[:, cols], ident[:])
-            hT_of[r] = hT
-
-        def group_h(r):
-            h_grouped = grouped_pool.tile([P, GROUP * E], BF16, align_bytes=64)
+        def group_a(s):
+            a_grouped = grouped_pool.tile([P, FFN], BF16, align_bytes=64)
             nc.scalar.copy(
-                out=h_grouped[:].bitcast(F32).rearrange("p (i r u) -> p i r u", i=GROUP, u=2),
-                in_=hT_of[r][:].rearrange("p (i u r) -> p i r u", i=GROUP, u=2),
+                out=a_grouped[:].bitcast(F32).rearrange("p (g r u) -> p g r u", g=DOWN_PASSES, u=2),
+                in_=aT_of[s][:].rearrange("p (g u r) -> p g r u", g=DOWN_PASSES, u=2),
             )
-            h_grouped_of[r] = h_grouped
+            a_grouped_of[s] = a_grouped
 
-        def quantise_h(r):
-            h_codes = mx_pool.tile([P, GROUP * P], U32, align_bytes=64)
-            h_scales = mx_pool.tile([P, GROUP * P], U8, align_bytes=64)
+        def quantise_a(s):
+            a_codes = mx_pool.tile([P, DOWN_PASSES * P], U32, align_bytes=64)
+            a_scales = mx_pool.tile([P, DOWN_PASSES * P], U8, align_bytes=64)
             nc.vector.quantize_mx(
-                out=h_codes[:].bitcast(FP8X4), scales=h_scales[:], in_=h_grouped_of[r][:]
+                out=a_codes[:].bitcast(FP8X4), scales=a_scales[:], in_=a_grouped_of[s][:]
             )
-            h_mx_of[r] = (h_codes, h_scales)
+            a_mx_of[s] = (a_codes, a_scales)
 
-        def project_kv(r):
-            h_codes, h_scales = h_mx_of[r]
-            kv_psum = psum_kv.tile([P, GROUP, 2 * KV], F32)
-            for i in range(GROUP):
-                cols = slice(i * P, (i + 1) * P)
+        def project_down(s):
+            a_codes, a_scales = a_mx_of[s]
+            x_psum = psum_x.tile([P, E], F32)
+            for g in range(DOWN_PASSES):
+                cols = slice(g * P, (g + 1) * P)
                 nc.tensor.matmul_mx(
-                    out=kv_psum[:, i, :],
-                    lhsT=h_codes[:, cols].bitcast(FP8X4),
-                    lhsT_scale=h_scales[:, cols],
-                    rhs=wkv_codes[:].bitcast(FP8X4),
-                    rhs_scale=wkv_scales[:],
-                    start=True,
-                    stop=True,
+                    out=x_psum[:],
+                    lhsT=a_codes[:, cols].bitcast(FP8X4),
+                    lhsT_scale=a_scales[:, cols],
+                    rhs=wd_codes[:, g, :].bitcast(FP8X4),
+                    rhs_scale=wd_scales[:, g, :],
+                    start=(g == 0),
+                    stop=(g == DOWN_PASSES - 1),
                 )
-            kv_psum_of[r] = kv_psum
+            x_psum_of[s] = x_psum
 
-        def store_kv(r):
-            c = r // ROUNDS_PER_CHUNK
-            if r % ROUNDS_PER_CHUNK == 0:
+        def add_residual(s):
+            if s % PAIR == 0:
+                x_sb = x_pool.tile([P, PAIR, E], F32)
+                x_of[s // PAIR] = x_sb
+            nc.vector.tensor_tensor(
+                out=x_of[s // PAIR][:, s % PAIR, :],
+                in0=x_psum_of[s][:],
+                in1=res_of[s // CHUNK_TILES][:, s % CHUNK_TILES, :],
+                op=ALU.add,
+            )
+            if s % PAIR == PAIR - 1:
+                nc.sync.dma_start(out=pair_view(x_rows, s - (PAIR - 1)), in_=x_of[s // PAIR][:])
+
+        def inverse_rms(s):
+            squares = square_pool.tile([P, E], BF16)
+            sum_sq = stat_pool.tile([P, 1], F32)
+            nc.scalar.activation(
+                out=squares[:], in_=x_of[s // PAIR][:, s % PAIR, :], func=ACT.Square, accum_out=sum_sq[:]
+            )
+            mean_sq = stat_pool.tile([P, 1], F32)
+            nc.gpsimd.tensor_scalar(
+                out=mean_sq[:], in0=sum_sq[:], scalar1=1.0 / E, scalar2=EPS, op0=ALU.mult, op1=ALU.add
+            )
+            rstd = stat_pool.tile([P, 1], F32)
+            nc.gpsimd.tensor_tensor(out=rstd[:], in0=mean_sq[:], in1=minus_half[:], op=ALU.pow)
+            rstd_of[s] = rstd
+
+        def normalise(s):
+            h_sb = h_pool.tile([P, E], BF16)
+            nc.vector.scalar_tensor_tensor(
+                out=h_sb[:],
+                in0=x_of[s // PAIR][:, s % PAIR, :],
+                scalar=rstd_of[s][:],
+                in1=gain[:],
+                op0=ALU.mult,
+                op1=ALU.mult,
+            )
+            h_of[s] = h_sb
+
+        def transpose_h(s):
+            h_words = h_of[s][:].bitcast(F32)
+            hT = psum_h.tile([P, 2 * P], F32)
+            for u in range(2):
+                cols = slice(u * P, (u + 1) * P)
+                nc.tensor.transpose(hT[:, cols], h_words[:, cols], ident[:])
+            hT_of[s] = hT
+
+        def group_h(s):
+            h_grouped = grouped_pool.tile([P, E], BF16, align_bytes=64)
+            nc.scalar.copy(
+                out=h_grouped[:].bitcast(F32).rearrange("p (r u) -> p r u", u=2),
+                in_=hT_of[s][:].rearrange("p (u r) -> p r u", u=2),
+            )
+            h_grouped_of[s] = h_grouped
+
+        def quantise_h(s):
+            h_codes = mx_pool.tile([P, P], U32, align_bytes=64)
+            h_scales = mx_pool.tile([P, P], U8, align_bytes=64)
+            nc.vector.quantize_mx(
+                out=h_codes[:].bitcast(FP8X4), scales=h_scales[:], in_=h_grouped_of[s][:]
+            )
+            h_mx_of[s] = (h_codes, h_scales)
+
+        def project_kv(s):
+            h_codes, h_scales = h_mx_of[s]
+            kv_psum = psum_kv.tile([P, 2 * KV], F32)
+            nc.tensor.matmul_mx(
+                out=kv_psum[:],
+                lhsT=h_codes[:].bitcast(FP8X4),
+                lhsT_scale=h_scales[:],
+                rhs=wkv_codes[:].bitcast(FP8X4),
+                rhs_scale=wkv_scales[:],
+                start=True,
+                stop=True,
+            )
+            kv_psum_of[s] = kv_psum
+
+        def store_kv(s):
+            c = s // CHUNK_TILES
+            if s % CHUNK_TILES == 0:
                 kv_sb = kv_pool.tile([P, 2, CHUNK_TILES, KV], F32)
                 kv_of[c] = kv_sb
-            j0 = first_tile(r)
             nc.scalar.copy(
-                out=kv_of[c][:, :, j0 : j0 + GROUP, :],
-                in_=kv_psum_of[r][:].rearrange("p i (s d) -> p s i d", s=2),
+                out=kv_of[c][:, :, s % CHUNK_TILES, :],
+                in_=kv_psum_of[s][:].rearrange("p (o d) -> p o d", o=2),
             )
-            if r % ROUNDS_PER_CHUNK == ROUNDS_PER_CHUNK - 1:
+            if s % CHUNK_TILES == CHUNK_TILES - 1:
                 nc.sync.dma_start(out=chunk_view(k_rows, c), in_=kv_of[c][:, 0])
                 nc.sync.dma_start(out=chunk_view(v_rows, c), in_=kv_of[c][:, 1])
 
-        def run(stage, r):
-            if 0 <= r < ROUNDS:
-                stage(r)
+        def run(stage, s):
+            if 0 <= s < TILES:
+                stage(s)
 
-        def frame(f):
-            run(load_round, f + 2 + LOADS_AHEAD)
-            run(transpose_h, f - 2)
-            run(add_residual, f)
-            run(root_mean_square, f)
-            run(transpose_a, f + 2)
-            run(quantise_a, f + 1)
-            run(project_down, f + 1)
-            run(normalise, f - 1)
-            run(group_h, f - 2)
-            run(store_kv, f - 3)
-            run(quantise_h, f - 2)
-            run(project_kv, f - 2)
-            run(group_a, f + 2)
+        def step(t):
+            run(load_inputs, t + 4 + LOADS_AHEAD)
+            run(transpose_h, t - 3)
+            run(transpose_a, t + 4)
+            run(add_residual, t)
+            run(inverse_rms, t)
+            run(normalise, t - 2)
+            run(group_a, t + 3)
+            run(group_h, t - 3)
+            run(store_kv, t - 5)
+            run(quantise_h, t - 4)
+            run(project_kv, t - 4)
+            run(quantise_a, t + 2)
+            run(project_down, t + 2)
 
-        frame(-2)
-        frame(-1)
+        for t in range(-4, 1):
+            step(t)
         quantise_wk_wv()
-        for f in range(ROUNDS + 3):
-            frame(f)
+        for t in range(1, TILES + 5):
+            step(t)

@@ -26,7 +26,6 @@ TILES = TOKENS // P
 PAIR = 2
 CHUNK_TILES = 4
 CHUNK = CHUNK_TILES * P
-LOADS_AHEAD = 8
 
 FLOPS = 2 * TOKENS * FFN * E + 2 * TOKENS * E * (2 * KV)
 
@@ -50,15 +49,15 @@ def tile_textencoderblock_pc_t_kernel(
 
     with ExitStack() as ctx:
         consts = ctx.enter_context(tc.tile_pool(name="consts", bufs=1))
-        a_pool = ctx.enter_context(tc.tile_pool(name="a", bufs=LOADS_AHEAD // PAIR + 2))
-        res_pool = ctx.enter_context(tc.tile_pool(name="res", bufs=5))
-        grouped_pool = ctx.enter_context(tc.tile_pool(name="grouped", bufs=2))
+        a_pool = ctx.enter_context(tc.tile_pool(name="a", bufs=TILES // PAIR))
+        res_pool = ctx.enter_context(tc.tile_pool(name="res", bufs=TILES // CHUNK_TILES))
+        grouped_pool = ctx.enter_context(tc.tile_pool(name="grouped", bufs=3))
         mx_pool = ctx.enter_context(tc.tile_pool(name="mx", bufs=2))
-        x_pool = ctx.enter_context(tc.tile_pool(name="x", bufs=4))
+        x_pool = ctx.enter_context(tc.tile_pool(name="x", bufs=10))
         stat_pool = ctx.enter_context(tc.tile_pool(name="stat", bufs=4))
         square_pool = ctx.enter_context(tc.tile_pool(name="square", bufs=4))
         h_pool = ctx.enter_context(tc.tile_pool(name="h", bufs=2))
-        kv_pool = ctx.enter_context(tc.tile_pool(name="kv", bufs=2))
+        kv_pool = ctx.enter_context(tc.tile_pool(name="kv", bufs=10))
         psum_gain = ctx.enter_context(tc.psum_pool(name="psum_gain", bufs=1))
         psum_a = ctx.enter_context(tc.psum_pool(name="psum_a", bufs=2))
         psum_x = ctx.enter_context(tc.psum_pool(name="psum_x", bufs=2))
@@ -86,29 +85,25 @@ def tile_textencoderblock_pc_t_kernel(
                 in_=rows.rearrange("(u p e) n -> p u (e n)", u=2, e=2),
             )
 
-        def load_inputs(s):
-            if s % PAIR == 0:
+        def load_chunk(c):
+            for s in range(c * CHUNK_TILES, (c + 1) * CHUNK_TILES, PAIR):
                 a_sb = a_pool.tile([P, PAIR, FFN], BF16)
                 nc.sync.dma_start(out=a_sb[:], in_=pair_view(a_rows, s))
                 a_of[s // PAIR] = a_sb
-            if s % CHUNK_TILES == 0:
-                res_sb = res_pool.tile([P, CHUNK_TILES, E], BF16)
-                nc.sync.dma_start(out=res_sb[:], in_=chunk_view(res_rows, s // CHUNK_TILES))
-                res_of[s // CHUNK_TILES] = res_sb
+            res_sb = res_pool.tile([P, CHUNK_TILES, E], BF16)
+            nc.sync.dma_start(out=res_sb[:], in_=chunk_view(res_rows, c))
+            res_of[c] = res_sb
 
         wd_raw = consts.tile([P, DOWN_PASSES, PACK, E], BF16)
         wkv_raw = consts.tile([P, 2, PACK, KV], BF16)
-        nc.sync.dma_start(out=gain_row[0:1, :], in_=ln1_w.unsqueeze(0))
         for g in range(DOWN_PASSES):
             load_weight_pass(wd[g * K_PASS : (g + 1) * K_PASS, :], wd_raw[:, g])
-        load_inputs(0)
+        load_chunk(0)
+        nc.sync.dma_start(out=gain_row[0:1, :], in_=ln1_w.unsqueeze(0))
         load_weight_pass(wk, wkv_raw[:, 0])
         load_weight_pass(wv, wkv_raw[:, 1])
-        for s in range(1, LOADS_AHEAD):
-            load_inputs(s)
-
-        gain = psum_gain.tile([P, E], F32)
-        nc.tensor.matmul(out=gain[:], lhsT=ones[:], rhs=gain_row[:], start=True, stop=True)
+        for c in range(1, TILES // CHUNK_TILES):
+            load_chunk(c)
 
         def group_weight(raw, grouped):
             nc.vector.tensor_copy(
@@ -132,7 +127,10 @@ def tile_textencoderblock_pc_t_kernel(
         wkv_codes = consts.tile([P, 2 * KV], U32, align_bytes=64)
         wkv_scales = consts.tile([P, 2 * KV], U8, align_bytes=64)
 
-        def quantise_wk_wv():
+        gain = psum_gain.tile([P, E], F32)
+
+        def prepare_norm_and_kv():
+            nc.tensor.matmul(out=gain[:], lhsT=ones[:], rhs=gain_row[:], start=True, stop=True)
             for s in range(2):
                 group_weight(wkv_raw[:, s], wkv_grouped[:, s])
             nc.vector.quantize_mx(
@@ -259,39 +257,37 @@ def tile_textencoderblock_pc_t_kernel(
             kv_psum_of[s] = kv_psum
 
         def store_kv(s):
-            c = s // CHUNK_TILES
-            if s % CHUNK_TILES == 0:
-                kv_sb = kv_pool.tile([P, 2, CHUNK_TILES, KV], F32)
-                kv_of[c] = kv_sb
+            if s % PAIR == 0:
+                kv_sb = kv_pool.tile([P, 2, PAIR, KV], F32)
+                kv_of[s // PAIR] = kv_sb
             nc.scalar.copy(
-                out=kv_of[c][:, :, s % CHUNK_TILES, :],
+                out=kv_of[s // PAIR][:, :, s % PAIR, :],
                 in_=kv_psum_of[s][:].rearrange("p (o d) -> p o d", o=2),
             )
-            if s % CHUNK_TILES == CHUNK_TILES - 1:
-                nc.sync.dma_start(out=chunk_view(k_rows, c), in_=kv_of[c][:, 0])
-                nc.sync.dma_start(out=chunk_view(v_rows, c), in_=kv_of[c][:, 1])
+            if s % PAIR == PAIR - 1:
+                nc.sync.dma_start(out=pair_view(k_rows, s - (PAIR - 1)), in_=kv_of[s // PAIR][:, 0])
+                nc.sync.dma_start(out=pair_view(v_rows, s - (PAIR - 1)), in_=kv_of[s // PAIR][:, 1])
 
         def run(stage, s):
             if 0 <= s < TILES:
                 stage(s)
 
         def step(t):
-            run(load_inputs, t + 4 + LOADS_AHEAD)
             run(transpose_h, t - 3)
-            run(transpose_a, t + 4)
+            run(transpose_a, t + 5)
             run(add_residual, t)
             run(inverse_rms, t)
+            run(quantise_h, t - 5)
             run(normalise, t - 2)
-            run(group_a, t + 3)
+            run(group_a, t + 4)
             run(group_h, t - 3)
-            run(store_kv, t - 5)
-            run(quantise_h, t - 4)
-            run(project_kv, t - 4)
+            run(store_kv, t - 6)
+            run(project_kv, t - 5)
             run(quantise_a, t + 2)
             run(project_down, t + 2)
 
-        for t in range(-4, 1):
+        for t in range(-5, 1):
             step(t)
-        quantise_wk_wv()
-        for t in range(1, TILES + 5):
+        prepare_norm_and_kv()
+        for t in range(1, TILES + 6):
             step(t)

@@ -49,14 +49,14 @@ def tile_textencoderblock_pc_t_kernel(
 
     with ExitStack() as ctx:
         consts = ctx.enter_context(tc.tile_pool(name="consts", bufs=1))
-        a_pool = ctx.enter_context(tc.tile_pool(name="a", bufs=TILES // PAIR))
+        a_pool = ctx.enter_context(tc.tile_pool(name="a", bufs=TILES))
         res_pool = ctx.enter_context(tc.tile_pool(name="res", bufs=TILES // CHUNK_TILES))
         grouped_pool = ctx.enter_context(tc.tile_pool(name="grouped", bufs=3))
         mx_pool = ctx.enter_context(tc.tile_pool(name="mx", bufs=2))
         x_pool = ctx.enter_context(tc.tile_pool(name="x", bufs=10))
         stat_pool = ctx.enter_context(tc.tile_pool(name="stat", bufs=4))
         square_pool = ctx.enter_context(tc.tile_pool(name="square", bufs=4))
-        h_pool = ctx.enter_context(tc.tile_pool(name="h", bufs=2))
+        h_pool = ctx.enter_context(tc.tile_pool(name="h", bufs=3))
         kv_pool = ctx.enter_context(tc.tile_pool(name="kv", bufs=10))
         psum_gain = ctx.enter_context(tc.psum_pool(name="psum_gain", bufs=1))
         psum_a = ctx.enter_context(tc.psum_pool(name="psum_a", bufs=2))
@@ -86,10 +86,10 @@ def tile_textencoderblock_pc_t_kernel(
             )
 
         def load_chunk(c):
-            for s in range(c * CHUNK_TILES, (c + 1) * CHUNK_TILES, PAIR):
-                a_sb = a_pool.tile([P, PAIR, FFN], BF16)
-                nc.sync.dma_start(out=a_sb[:], in_=pair_view(a_rows, s))
-                a_of[s // PAIR] = a_sb
+            for j in range(CHUNK_TILES):
+                a_sb = a_pool.tile([P, FFN], BF16)
+                nc.sync.dma_start(out=a_sb[:], in_=chunk_view(a_rows, c)[:, j, :])
+                a_of[c * CHUNK_TILES + j] = a_sb
             res_sb = res_pool.tile([P, CHUNK_TILES, E], BF16)
             nc.sync.dma_start(out=res_sb[:], in_=chunk_view(res_rows, c))
             res_of[c] = res_sb
@@ -140,7 +140,7 @@ def tile_textencoderblock_pc_t_kernel(
             )
 
         def transpose_a(s):
-            a_words = a_of[s // PAIR][:, s % PAIR, :].bitcast(F32)
+            a_words = a_of[s][:].bitcast(F32)
             aT = psum_a.tile([P, PACK * P], F32)
             for gu in range(PACK):
                 cols = slice(gu * P, (gu + 1) * P)

@@ -260,10 +260,12 @@ def tile_textencoderblock_pc_t_kernel(
             if s % PAIR == 0:
                 kv_sb = kv_pool.tile([P, 2, PAIR, KV], F32)
                 kv_of[s // PAIR] = kv_sb
-            nc.scalar.copy(
-                out=kv_of[s // PAIR][:, :, s % PAIR, :],
-                in_=kv_psum_of[s][:].rearrange("p (o d) -> p o d", o=2),
-            )
+            kv_out = kv_of[s // PAIR][:, :, s % PAIR, :]
+            kv_in = kv_psum_of[s][:].rearrange("p (o d) -> p o d", o=2)
+            if s % CHUNK_TILES == CHUNK_TILES - 1:
+                nc.vector.tensor_copy(out=kv_out, in_=kv_in)
+            else:
+                nc.scalar.copy(out=kv_out, in_=kv_in)
             if s % PAIR == PAIR - 1:
                 nc.sync.dma_start(out=pair_view(k_rows, s - (PAIR - 1)), in_=kv_of[s // PAIR][:, 0])
                 nc.sync.dma_start(out=pair_view(v_rows, s - (PAIR - 1)), in_=kv_of[s // PAIR][:, 1])

from contextlib import ExitStack

import concourse.mybir as mybir
from concourse.masks import make_identity

F32 = mybir.dt.float32
BF16 = mybir.dt.bfloat16
U32 = mybir.dt.uint32
U8 = mybir.dt.uint8
FP8X4 = mybir.dt.float8_e4m3fn_x4
ACT = mybir.ActivationFunctionType
ALU = mybir.AluOpType

P = 128
PACK = 4
K_PASS = P * PACK

TOKENS = 4096
FFN = 1024
E = 512
KV = 128
EPS = 2.0**-23
DOWN_PASSES = FFN // K_PASS

TILES = TOKENS // P
PAIR = 2
CHUNK_TILES = 4
CHUNK = CHUNK_TILES * P

FLOPS = 2 * TOKENS * FFN * E + 2 * TOKENS * E * (2 * KV)


def tile_textencoderblock_pc_t_kernel(
    tc, ffn_act, wd, residual, ln1_w, wk, wv, out_0, out_1, out_2
):
    nc = tc.nc
    a_rows = ffn_act.flatten_outer_dims()
    res_rows = residual.flatten_outer_dims()
    x_rows = out_0.flatten_outer_dims()
    k_rows = out_1.flatten_outer_dims()
    v_rows = out_2.flatten_outer_dims()

    def chunk_view(rows, c):
        return rows[c * CHUNK : (c + 1) * CHUNK, :].rearrange("(p j) w -> p j w", j=CHUNK_TILES)

    def pair_view(rows, s):
        j0 = s % CHUNK_TILES
        return chunk_view(rows, s // CHUNK_TILES)[:, j0 : j0 + PAIR, :]

    with ExitStack() as ctx:
        consts = ctx.enter_context(tc.tile_pool(name="consts", bufs=1))
        a_pool = ctx.enter_context(tc.tile_pool(name="a", bufs=TILES))
        res_pool = ctx.enter_context(tc.tile_pool(name="res", bufs=TILES // CHUNK_TILES))
        grouped_pool = ctx.enter_context(tc.tile_pool(name="grouped", bufs=3))
        mx_pool = ctx.enter_context(tc.tile_pool(name="mx", bufs=2))
        x_pool = ctx.enter_context(tc.tile_pool(name="x", bufs=10))
        stat_pool = ctx.enter_context(tc.tile_pool(name="stat", bufs=4))
        square_pool = ctx.enter_context(tc.tile_pool(name="square", bufs=4))
        h_pool = ctx.enter_context(tc.tile_pool(name="h", bufs=3))
        kv_pool = ctx.enter_context(tc.tile_pool(name="kv", bufs=10))
        psum_gain = ctx.enter_context(tc.psum_pool(name="psum_gain", bufs=1))
        psum_a = ctx.enter_context(tc.psum_pool(name="psum_a", bufs=2))
        psum_x = ctx.enter_context(tc.psum_pool(name="psum_x", bufs=2))
        psum_h = ctx.enter_context(tc.psum_pool(name="psum_h", bufs=1))
        psum_kv = ctx.enter_context(tc.psum_pool(name="psum_kv", bufs=2))
        ctx.enter_context(tc.manual_schedule())

        a_of, res_of, aT_of, a_grouped_of, a_mx_of, x_psum_of, x_of = {}, {}, {}, {}, {}, {}, {}
        rstd_of, h_of, hT_of, h_grouped_of, h_mx_of, kv_psum_of, kv_of = {}, {}, {}, {}, {}, {}, {}

        ident = consts.tile([P, P], F32)
        make_identity(nc, ident[:])
        ones = consts.tile([P, P], BF16)
        nc.vector.memset(ones[:], 1.0)
        gain_row = consts.tile([P, E], BF16)
        nc.vector.memset(gain_row[:], 0.0)
        minus_half = consts.tile([P, 1], F32)
        nc.vector.memset(minus_half[:], -0.5)
        table_warmer = consts.tile([P, 1], F32)
        nc.scalar.activation(out=table_warmer[:], in_=minus_half[:], func=ACT.Square)

        def load_weight_pass(rows, raw):
            nc.sync.dma_start(
                out=raw.rearrange("p (u e) n -> p u (e n)", e=2),
                in_=rows.rearrange("(u p e) n -> p u (e n)", u=2, e=2),
            )

        def load_chunk(c):
            for j in range(CHUNK_TILES):
                a_sb = a_pool.tile([P, FFN], BF16)
                nc.sync.dma_start(out=a_sb[:], in_=chunk_view(a_rows, c)[:, j, :])
                a_of[c * CHUNK_TILES + j] = a_sb
            res_sb = res_pool.tile([P, CHUNK_TILES, E], BF16)
            nc.sync.dma_start(out=res_sb[:], in_=chunk_view(res_rows, c))
            res_of[c] = res_sb

        wd_raw = consts.tile([P, DOWN_PASSES, PACK, E], BF16)
        wkv_raw = consts.tile([P, 2, PACK, KV], BF16)
        for g in range(DOWN_PASSES):
            load_weight_pass(wd[g * K_PASS : (g + 1) * K_PASS, :], wd_raw[:, g])
        load_chunk(0)
        nc.sync.dma_start(out=gain_row[0:1, :], in_=ln1_w.unsqueeze(0))
        load_weight_pass(wk, wkv_raw[:, 0])
        load_weight_pass(wv, wkv_raw[:, 1])
        for c in range(1, TILES // CHUNK_TILES):
            load_chunk(c)

        def group_weight(raw, grouped):
            nc.vector.tensor_copy(
                out=grouped.rearrange("p (c i) t -> p c t i", i=4),
                in_=raw.rearrange("p t (c i) -> p c t i", i=4),
            )

        wd_grouped = consts.tile([P, DOWN_PASSES, E, PACK], BF16, align_bytes=64)
        wd_codes = consts.tile([P, DOWN_PASSES, E], U32, align_bytes=64)
        wd_scales = consts.tile([P, DOWN_PASSES, E], U8, align_bytes=64)
        for g in range(DOWN_PASSES):
            group_weight(wd_raw[:, g], wd_grouped[:, g])
        for g in range(DOWN_PASSES):
            nc.vector.quantize_mx(
                out=wd_codes[:, g, :].bitcast(FP8X4),
                scales=wd_scales[:, g, :],
                in_=wd_grouped[:, g].rearrange("p n t -> p (n t)"),
            )

        wkv_grouped = consts.tile([P, 2, KV, PACK], BF16, align_bytes=64)
        wkv_codes = consts.tile([P, 2 * KV], U32, align_bytes=64)
        wkv_scales = consts.tile([P, 2 * KV], U8, align_bytes=64)

        gain = psum_gain.tile([P, E], F32)

        def prepare_norm_and_kv():
            nc.tensor.matmul(out=gain[:], lhsT=ones[:], rhs=gain_row[:], start=True, stop=True)
            for s in range(2):
                group_weight(wkv_raw[:, s], wkv_grouped[:, s])
            nc.vector.quantize_mx(
                out=wkv_codes[:].bitcast(FP8X4),
                scales=wkv_scales[:],
                in_=wkv_grouped[:].rearrange("p s n t -> p (s n t)"),
            )

        def transpose_a(s):
            a_words = a_of[s][:].bitcast(F32)
            aT = psum_a.tile([P, PACK * P], F32)
            for gu in range(PACK):
                cols = slice(gu * P, (gu + 1) * P)
                nc.tensor.transpose(aT[:, cols], a_words[:, cols], ident[:])
            aT_of[s] = aT

        def group_a(s):
            a_grouped = grouped_pool.tile([P, FFN], BF16, align_bytes=64)
            nc.scalar.copy(
                out=a_grouped[:].bitcast(F32).rearrange("p (g r u) -> p g r u", g=DOWN_PASSES, u=2),
                in_=aT_of[s][:].rearrange("p (g u r) -> p g r u", g=DOWN_PASSES, u=2),
            )
            a_grouped_of[s] = a_grouped

        def quantise_a(s):
            a_codes = mx_pool.tile([P, DOWN_PASSES * P], U32, align_bytes=64)
            a_scales = mx_pool.tile([P, DOWN_PASSES * P], U8, align_bytes=64)
            nc.vector.quantize_mx(
                out=a_codes[:].bitcast(FP8X4), scales=a_scales[:], in_=a_grouped_of[s][:]
            )
            a_mx_of[s] = (a_codes, a_scales)

        def project_down(s):
            a_codes, a_scales = a_mx_of[s]
            x_psum = psum_x.tile([P, E], F32)
            for g in range(DOWN_PASSES):
                cols = slice(g * P, (g + 1) * P)
                nc.tensor.matmul_mx(
                    out=x_psum[:],
                    lhsT=a_codes[:, cols].bitcast(FP8X4),
                    lhsT_scale=a_scales[:, cols],
                    rhs=wd_codes[:, g, :].bitcast(FP8X4),
                    rhs_scale=wd_scales[:, g, :],
                    start=(g == 0),
                    stop=(g == DOWN_PASSES - 1),
                )
            x_psum_of[s] = x_psum

        def add_residual(s):
            if s % PAIR == 0:
                x_sb = x_pool.tile([P, PAIR, E], F32)
                x_of[s // PAIR] = x_sb
            nc.vector.tensor_tensor(
                out=x_of[s // PAIR][:, s % PAIR, :],
                in0=x_psum_of[s][:],
                in1=res_of[s // CHUNK_TILES][:, s % CHUNK_TILES, :],
                op=ALU.add,
            )
            if s % PAIR == PAIR - 1:
                nc.sync.dma_start(out=pair_view(x_rows, s - (PAIR - 1)), in_=x_of[s // PAIR][:])

        def inverse_rms(s):
            squares = square_pool.tile([P, E], BF16)
            sum_sq = stat_pool.tile([P, 1], F32)
            nc.scalar.activation(
                out=squares[:], in_=x_of[s // PAIR][:, s % PAIR, :], func=ACT.Square, accum_out=sum_sq[:]
            )
            mean_sq = stat_pool.tile([P, 1], F32)
            nc.gpsimd.tensor_scalar(
                out=mean_sq[:], in0=sum_sq[:], scalar1=1.0 / E, scalar2=EPS, op0=ALU.mult, op1=ALU.add
            )
            rstd = stat_pool.tile([P, 1], F32)
            nc.gpsimd.tensor_tensor(out=rstd[:], in0=mean_sq[:], in1=minus_half[:], op=ALU.pow)
            rstd_of[s] = rstd

        def normalise(s):
            h_sb = h_pool.tile([P, E], BF16)
            nc.vector.scalar_tensor_tensor(
                out=h_sb[:],
                in0=x_of[s // PAIR][:, s % PAIR, :],
                scalar=rstd_of[s][:],
                in1=gain[:],
                op0=ALU.mult,
                op1=ALU.mult,
            )
            h_of[s] = h_sb

        def transpose_h(s):
            h_words = h_of[s][:].bitcast(F32)
            hT = psum_h.tile([P, 2 * P], F32)
            for u in range(2):
                cols = slice(u * P, (u + 1) * P)
                nc.tensor.transpose(hT[:, cols], h_words[:, cols], ident[:])
            hT_of[s] = hT

        def group_h(s):
            h_grouped = grouped_pool.tile([P, E], BF16, align_bytes=64)
            nc.scalar.copy(
                out=h_grouped[:].bitcast(F32).rearrange("p (r u) -> p r u", u=2),
                in_=hT_of[s][:].rearrange("p (u r) -> p r u", u=2),
            )
            h_grouped_of[s] = h_grouped

        def quantise_h(s):
            h_codes = mx_pool.tile([P, P], U32, align_bytes=64)
            h_scales = mx_pool.tile([P, P], U8, align_bytes=64)
            nc.vector.quantize_mx(
                out=h_codes[:].bitcast(FP8X4), scales=h_scales[:], in_=h_grouped_of[s][:]
            )
            h_mx_of[s] = (h_codes, h_scales)

        def project_kv(s):
            h_codes, h_scales = h_mx_of[s]
            kv_psum = psum_kv.tile([P, 2 * KV], F32)
            nc.tensor.matmul_mx(
                out=kv_psum[:],
                lhsT=h_codes[:].bitcast(FP8X4),
                lhsT_scale=h_scales[:],
                rhs=wkv_codes[:].bitcast(FP8X4),
                rhs_scale=wkv_scales[:],
                start=True,
                stop=True,
            )
            kv_psum_of[s] = kv_psum

        def store_kv(s):
            if s % PAIR == 0:
                kv_sb = kv_pool.tile([P, 2, PAIR, KV], F32)
                kv_of[s // PAIR] = kv_sb
            kv_out = kv_of[s // PAIR][:, :, s % PAIR, :]
            kv_in = kv_psum_of[s][:].rearrange("p (o d) -> p o d", o=2)
            if s % CHUNK_TILES == CHUNK_TILES - 1:
                nc.vector.tensor_copy(out=kv_out, in_=kv_in)
            else:
                nc.scalar.copy(out=kv_out, in_=kv_in)
            if s % PAIR == PAIR - 1:
                nc.sync.dma_start(out=pair_view(k_rows, s - (PAIR - 1)), in_=kv_of[s // PAIR][:, 0])
                nc.sync.dma_start(out=pair_view(v_rows, s - (PAIR - 1)), in_=kv_of[s // PAIR][:, 1])

        def run(stage, s):
            if 0 <= s < TILES:
                stage(s)

        def step(t):
            run(transpose_h, t - 3)
            run(transpose_a, t + 5)
            run(add_residual, t)
            run(inverse_rms, t)
            run(quantise_h, t - 5)
            run(normalise, t - 2)
            run(group_a, t + 4)
            run(group_h, t - 3)
            run(store_kv, t - 6)
            run(project_kv, t - 5)
            run(quantise_a, t + 2)
            run(project_down, t + 2)

        for t in range(-5, 1):
            step(t)
        prepare_norm_and_kv()
        for t in range(1, TILES + 6):
            step(t)
